import numpy as np
import ml_dtypes


def mxq(x, axis, fmt="e4m3"):
    dtype, down = {"e4m3": (ml_dtypes.float8_e4m3fn, 7), "e5m2": (ml_dtypes.float8_e5m2, 14)}[fmt]
    v = np.moveaxis(np.asarray(x, np.float32).astype(ml_dtypes.bfloat16).astype(np.float64), axis, -1)
    blocks = v.reshape(v.shape[:-1] + (-1, 32))
    amax = np.abs(blocks).max(-1, keepdims=True)
    byte = np.maximum(np.where(amax > 0, np.frexp(amax)[1] - 1 + 127, 0) - down, 1)
    scale = np.exp2(byte - 127.0)
    codes = (blocks / scale).astype(np.float32).astype(dtype).astype(np.float64)
    return np.moveaxis((codes * scale).reshape(v.shape), -1, axis)


WIDE = False


def mx_kscale(k):
    if not WIDE:
        return np.ones(k)
    levels = np.array([20, -20, 10, -10, 0])
    a = np.random.permutation(np.resize(levels, k // 512 * 4)).reshape(k // 512, 4)
    idx = np.arange(k)
    return np.exp2(a[idx // 512, idx % 128 // 32])


BF16 = ml_dtypes.bfloat16


def bf(x):
    return np.asarray(x, np.float32).astype(BF16)


def f64(x):
    return np.asarray(x).astype(np.float64)


N, LMAX, CIN, COUT = 512, 1, 128, 8192
NL = LMAX + 1
NM = NL * NL


def setup_inputs():
    u = mx_kscale(COUT)
    x = np.random.standard_normal((N, NM, CIN))
    weights = np.random.standard_normal((NL, CIN, COUT)) / np.sqrt(CIN) / u
    path_weights = 1.0 + 0.3 * np.random.standard_normal(NL)
    g = np.random.standard_normal((N, NM, COUT)) * np.exp2(np.random.randint(-12, 1, (N, NM, 1))) * 16.0 * u
    return {"x": bf(x), "weights": bf(weights), "path_weights": bf(path_weights), "grad_out": bf(g)}


def reference(x, weights, path_weights, grad_out):
    weights, path_weights, g = f64(weights), f64(path_weights), f64(grad_out)
    blocks = []
    for l in range(LMAX + 1):
        start = l * l
        end = start + (2 * l + 1)
        blk = mxq(g[:, start:end, :], 2, "e5m2") @ mxq(weights[l], 1, "e4m3").T
        blocks.append(path_weights[l] * blk)
    return np.concatenate(blocks, axis=1)

@@ -1,0 +1,176 @@
+from contextlib import ExitStack
+
+import concourse.mybir as mybir
+from concourse.masks import make_identity
+
+BF16 = mybir.dt.bfloat16
+F32 = mybir.dt.float32
+U32 = mybir.dt.uint32
+U8 = mybir.dt.uint8
+E4M3X4 = mybir.dt.float8_e4m3fn_x4
+E5M2X4 = mybir.dt.float8_e5m2_x4
+
+P = 128
+PACK = 4
+K_PASS = P * PACK
+PAIRS = K_PASS // 2
+
+NODES = 512
+ROWS = 4
+DEGREE_OF_ROW = [0, 1, 1, 1]
+DEGREES = 2
+C_IN = 128
+K = 8192
+PASSES = K // K_PASS
+NODE_TILES = NODES // P
+BLOCKS = 4
+
+CHUNK_PASSES = 4
+CHUNK_K = CHUNK_PASSES * K_PASS
+CHUNKS = PASSES // CHUNK_PASSES
+
+FLOPS = 2 * NODES * ROWS * K * C_IN
+BYTES = 2 * (DEGREES * C_IN * K + NODES * ROWS * K + DEGREES) + 4 * NODES * ROWS * C_IN
+
+
+def tile_linear_pa_k_kernel(tc, x, weights, path_weights, grad_out, out):
+    nc = tc.nc
+    with ExitStack() as ctx:
+        consts = ctx.enter_context(tc.tile_pool(name="consts", bufs=1))
+        w_raw_pool = ctx.enter_context(tc.tile_pool(name="w_raw", bufs=2))
+        g_raw_pool = ctx.enter_context(tc.tile_pool(name="g_raw", bufs=6))
+        grouped_pool = ctx.enter_context(tc.tile_pool(name="grouped", bufs=4))
+        g_mx_pool = ctx.enter_context(tc.tile_pool(name="g_mx", bufs=3))
+        out_pool = ctx.enter_context(tc.tile_pool(name="out", bufs=2))
+        bank_pool = ctx.enter_context(tc.psum_pool(name="bank", bufs=6))
+        acc_pool = ctx.enter_context(tc.psum_pool(name="acc", bufs=2))
+        ctx.enter_context(tc.manual_schedule())
+
+        ident = consts.tile([P, P], F32)
+        make_identity(nc, ident[:])
+
+        pw_bf16 = consts.tile([P, DEGREES], BF16)
+        nc.scalar.dma_start(out=pw_bf16[:], in_=path_weights.partition_broadcast(P))
+        pw = consts.tile([P, DEGREES], F32)
+        nc.vector.tensor_copy(out=pw[:], in_=pw_bf16[:])
+
+        def transpose_blocks(blocks, vector_helps):
+            grouped = grouped_pool.tile([P, BLOCKS * P * PACK], BF16, align_bytes=64)
+            grouped_words = grouped[:].bitcast(F32).rearrange("p (b r u) -> p b r u", b=BLOCKS, u=2)
+            for half in range(2):
+                bank = bank_pool.tile([P, 2, 2, P], F32, tag="bank")
+                for b in range(2):
+                    for u in range(2):
+                        nc.tensor.transpose(
+                            bank[:, b, u, :], blocks[2 * half + b][:, u * P : (u + 1) * P], ident[:]
+                        )
+                dst = grouped_words[:, 2 * half : 2 * half + 2, :, :]
+                src = bank[:].rearrange("p b u r -> p b r u")
+                if half == 1 and vector_helps:
+                    nc.vector.tensor_copy(out=dst, in_=src)
+                else:
+                    nc.scalar.copy(out=dst, in_=src)
+            return grouped
+
+        def transpose_and_quantise(block_lists, codes, scales, fmt):
+            waiting = []
+            for i in range(len(block_lists)):
+                waiting.append(transpose_blocks(block_lists[i], vector_helps=(i % 2 == 1)))
+                if i >= 1:
+                    nc.vector.quantize_mx(
+                        out=codes[i - 1].bitcast(fmt), scales=scales[i - 1], in_=waiting[i - 1][:]
+                    )
+            last = len(block_lists) - 1
+            nc.vector.quantize_mx(out=codes[last].bitcast(fmt), scales=scales[last], in_=waiting[last][:])
+
+        def prepare_weights(degree):
+            w_raw = w_raw_pool.tile([P, K], BF16)
+            nc.sync.dma_start(out=w_raw[:], in_=weights[degree])
+            w_words = w_raw[:].bitcast(F32)
+            w_codes = consts.tile([P, PASSES * C_IN], U32, align_bytes=64, name="w_codes%d" % degree)
+            w_scales = consts.tile([P, PASSES * C_IN], U8, align_bytes=64, name="w_scales%d" % degree)
+            width = BLOCKS * C_IN
+            calls = PASSES // BLOCKS
+            transpose_and_quantise(
+                [
+                    [w_words[:, (BLOCKS * q + i) * PAIRS : (BLOCKS * q + i + 1) * PAIRS] for i in range(BLOCKS)]
+                    for q in range(calls)
+                ],
+                [w_codes[:, q * width : (q + 1) * width] for q in range(calls)],
+                [w_scales[:, q * width : (q + 1) * width] for q in range(calls)],
+                E4M3X4,
+            )
+            return w_codes, w_scales
+
+        def prepare_chunk(row, chunk):
+            g_raw = g_raw_pool.tile([P, NODE_TILES, CHUNK_K], BF16)
+            nc.sync.dma_start(
+                out=g_raw[:],
+                in_=grad_out[:, row, chunk * CHUNK_K : (chunk + 1) * CHUNK_K].rearrange(
+                    "(t p) k -> p t k", p=P
+                ),
+            )
+            g_words = g_raw[:].bitcast(F32)
+            g_codes = g_mx_pool.tile([P, CHUNK_PASSES, NODES], U32, align_bytes=64)
+            g_scales = g_mx_pool.tile([P, CHUNK_PASSES, NODES], U8, align_bytes=64)
+            transpose_and_quantise(
+                [
+                    [g_words[:, t, c * PAIRS : (c + 1) * PAIRS] for t in range(NODE_TILES)]
+                    for c in range(CHUNK_PASSES)
+                ],
+                [g_codes[:, c, :] for c in range(CHUNK_PASSES)],
+                [g_scales[:, c, :] for c in range(CHUNK_PASSES)],
+                E5M2X4,
+            )
+            return g_codes, g_scales
+
+        def multiply(acc, chunk, w_codes, w_scales, g_codes, g_scales):
+            for c in range(CHUNK_PASSES):
+                k_pass = chunk * CHUNK_PASSES + c
+                nc.tensor.matmul_mx(
+                    out=acc[:],
+                    lhsT=w_codes[:, k_pass * C_IN : (k_pass + 1) * C_IN].bitcast(E4M3X4),
+                    lhsT_scale=w_scales[:, k_pass * C_IN : (k_pass + 1) * C_IN],
+                    rhs=g_codes[:, c, :].bitcast(E5M2X4),
+                    rhs_scale=g_scales[:, c, :],
+                    start=(k_pass == 0),
+                    stop=(k_pass == PASSES - 1),
+                )
+
+        def write_out(row, acc):
+            degree = DEGREE_OF_ROW[row]
+            scaled = out_pool.tile([P, NODES], F32)
+            nc.vector.tensor_scalar(
+                out=scaled[:],
+                in0=acc[:],
+                scalar1=pw[:, degree : degree + 1],
+                scalar2=None,
+                op0=mybir.AluOpType.mult,
+            )
+            back = bank_pool.tile([P, NODE_TILES, C_IN], F32, tag="bank")
+            for t in range(NODE_TILES):
+                nc.tensor.transpose(back[:, t, :], scaled[:, t * P : (t + 1) * P], ident[:])
+            result = out_pool.tile([P, NODE_TILES, C_IN], F32)
+            nc.scalar.copy(out=result[:], in_=back[:])
+            nc.scalar.dma_start(out=out[:, row, :].rearrange("(t p) c -> p t c", p=P), in_=result[:])
+
+        steps = [(row, chunk) for row in range(ROWS) for chunk in range(CHUNKS)]
+        w_mx = {}
+        g_mx = {}
+        acc_of_row = {}
+        for i in range(len(steps) + 1):
+            if i < len(steps):
+                row, chunk = steps[i]
+                degree = DEGREE_OF_ROW[row]
+                if degree not in w_mx:
+                    w_mx[degree] = prepare_weights(degree)
+                g_mx[i] = prepare_chunk(row, chunk)
+            if i >= 1:
+                row, chunk = steps[i - 1]
+                if chunk == 0:
+                    acc_of_row[row] = acc_pool.tile([P, NODES], F32, name="acc")
+                w_codes, w_scales = w_mx[DEGREE_OF_ROW[row]]
+                g_codes, g_scales = g_mx[i - 1]
+                multiply(acc_of_row[row], chunk, w_codes, w_scales, g_codes, g_scales)
+                if chunk == CHUNKS - 1:
+                    write_out(row, acc_of_row[row])

@@ -25,25 +25,47 @@ PASSES = K // K_PASS
 NODE_TILES = NODES // P
 BLOCKS = 4
 
-CHUNK_PASSES = 4
-CHUNK_K = CHUNK_PASSES * K_PASS
-CHUNKS = PASSES // CHUNK_PASSES
+LOAD_PASSES = 8
 
 FLOPS = 2 * NODES * ROWS * K * C_IN
 BYTES = 2 * (DEGREES * C_IN * K + NODES * ROWS * K + DEGREES) + 4 * NODES * ROWS * C_IN
+
+
+def halved_down_to_one(passes):
+    pieces = []
+    while passes > 1:
+        passes //= 2
+        pieces.append(passes)
+    return pieces + [1]
+
+
+def loads_of_grad_out():
+    taper = halved_down_to_one(LOAD_PASSES)
+    loads = []
+    for row in range(ROWS):
+        sizes = [LOAD_PASSES] * (PASSES // LOAD_PASSES)
+        if row == 0:
+            sizes = list(reversed(taper)) + sizes[1:]
+        if row == ROWS - 1:
+            sizes = sizes[:-1] + taper
+        first = 0
+        for passes in sizes:
+            loads.append((row, first, passes))
+            first += passes
+    return loads
 
 
 def tile_linear_pa_k_kernel(tc, x, weights, path_weights, grad_out, out):
     nc = tc.nc
     with ExitStack() as ctx:
         consts = ctx.enter_context(tc.tile_pool(name="consts", bufs=1))
-        w_raw_pool = ctx.enter_context(tc.tile_pool(name="w_raw", bufs=2))
-        g_raw_pool = ctx.enter_context(tc.tile_pool(name="g_raw", bufs=6))
+        w_raw_pool = ctx.enter_context(tc.tile_pool(name="w_raw", bufs=4))
+        g_raw_pool = ctx.enter_context(tc.tile_pool(name="g_raw", bufs=4))
         grouped_pool = ctx.enter_context(tc.tile_pool(name="grouped", bufs=4))
-        g_mx_pool = ctx.enter_context(tc.tile_pool(name="g_mx", bufs=3))
+        g_mx_pool = ctx.enter_context(tc.tile_pool(name="g_mx", bufs=2))
         out_pool = ctx.enter_context(tc.tile_pool(name="out", bufs=2))
-        bank_pool = ctx.enter_context(tc.psum_pool(name="bank", bufs=6))
-        acc_pool = ctx.enter_context(tc.psum_pool(name="acc", bufs=2))
+        bank_pool = ctx.enter_context(tc.psum_pool(name="bank", bufs=7))
+        acc_pool = ctx.enter_context(tc.psum_pool(name="acc", bufs=1))
         ctx.enter_context(tc.manual_schedule())
 
         ident = consts.tile([P, P], F32)
@@ -72,10 +94,10 @@ def tile_linear_pa_k_kernel(tc, x, weights, path_weights, grad_out, out):
                     nc.scalar.copy(out=dst, in_=src)
             return grouped
 
-        def transpose_and_quantise(block_lists, codes, scales, fmt):
+        def transpose_and_quantise(first, block_lists, codes, scales, fmt):
             waiting = []
             for i in range(len(block_lists)):
-                waiting.append(transpose_blocks(block_lists[i], vector_helps=(i % 2 == 1)))
+                waiting.append(transpose_blocks(block_lists[i], vector_helps=((first + i) % 2 == 1)))
                 if i >= 1:
                     nc.vector.quantize_mx(
                         out=codes[i - 1].bitcast(fmt), scales=scales[i - 1], in_=waiting[i - 1][:]
@@ -84,49 +106,49 @@ def tile_linear_pa_k_kernel(tc, x, weights, path_weights, grad_out, out):
             nc.vector.quantize_mx(out=codes[last].bitcast(fmt), scales=scales[last], in_=waiting[last][:])
 
         def prepare_weights(degree):
-            w_raw = w_raw_pool.tile([P, K], BF16)
-            nc.sync.dma_start(out=w_raw[:], in_=weights[degree])
-            w_words = w_raw[:].bitcast(F32)
-            w_codes = consts.tile([P, PASSES * C_IN], U32, align_bytes=64, name="w_codes%d" % degree)
-            w_scales = consts.tile([P, PASSES * C_IN], U8, align_bytes=64, name="w_scales%d" % degree)
             width = BLOCKS * C_IN
             calls = PASSES // BLOCKS
+            w_words = []
+            for q in range(calls):
+                w_raw = w_raw_pool.tile([P, BLOCKS * K_PASS], BF16)
+                nc.sync.dma_start(
+                    out=w_raw[:], in_=weights[degree, :, q * BLOCKS * K_PASS : (q + 1) * BLOCKS * K_PASS]
+                )
+                w_words.append(w_raw[:].bitcast(F32))
+            w_codes = consts.tile([P, PASSES * C_IN], U32, align_bytes=64, name="w_codes%d" % degree)
+            w_scales = consts.tile([P, PASSES * C_IN], U8, align_bytes=64, name="w_scales%d" % degree)
             transpose_and_quantise(
-                [
-                    [w_words[:, (BLOCKS * q + i) * PAIRS : (BLOCKS * q + i + 1) * PAIRS] for i in range(BLOCKS)]
-                    for q in range(calls)
-                ],
+                0,
+                [[w_words[q][:, i * PAIRS : (i + 1) * PAIRS] for i in range(BLOCKS)] for q in range(calls)],
                 [w_codes[:, q * width : (q + 1) * width] for q in range(calls)],
                 [w_scales[:, q * width : (q + 1) * width] for q in range(calls)],
                 E4M3X4,
             )
             return w_codes, w_scales
 
-        def prepare_chunk(row, chunk):
-            g_raw = g_raw_pool.tile([P, NODE_TILES, CHUNK_K], BF16)
+        def prepare_grad_out(row, first, passes):
+            g_raw = g_raw_pool.tile([P, NODE_TILES, passes * K_PASS], BF16)
             nc.sync.dma_start(
                 out=g_raw[:],
-                in_=grad_out[:, row, chunk * CHUNK_K : (chunk + 1) * CHUNK_K].rearrange(
+                in_=grad_out[:, row, first * K_PASS : (first + passes) * K_PASS].rearrange(
                     "(t p) k -> p t k", p=P
                 ),
             )
             g_words = g_raw[:].bitcast(F32)
-            g_codes = g_mx_pool.tile([P, CHUNK_PASSES, NODES], U32, align_bytes=64)
-            g_scales = g_mx_pool.tile([P, CHUNK_PASSES, NODES], U8, align_bytes=64)
+            g_codes = g_mx_pool.tile([P, passes, NODES], U32, align_bytes=64)
+            g_scales = g_mx_pool.tile([P, passes, NODES], U8, align_bytes=64)
             transpose_and_quantise(
-                [
-                    [g_words[:, t, c * PAIRS : (c + 1) * PAIRS] for t in range(NODE_TILES)]
-                    for c in range(CHUNK_PASSES)
-                ],
-                [g_codes[:, c, :] for c in range(CHUNK_PASSES)],
-                [g_scales[:, c, :] for c in range(CHUNK_PASSES)],
+                first,
+                [[g_words[:, t, c * PAIRS : (c + 1) * PAIRS] for t in range(NODE_TILES)] for c in range(passes)],
+                [g_codes[:, c, :] for c in range(passes)],
+                [g_scales[:, c, :] for c in range(passes)],
                 E5M2X4,
             )
             return g_codes, g_scales
 
-        def multiply(acc, chunk, w_codes, w_scales, g_codes, g_scales):
-            for c in range(CHUNK_PASSES):
-                k_pass = chunk * CHUNK_PASSES + c
+        def multiply(acc, first, passes, w_codes, w_scales, g_codes, g_scales):
+            for c in range(passes):
+                k_pass = first + c
                 nc.tensor.matmul_mx(
                     out=acc[:],
                     lhsT=w_codes[:, k_pass * C_IN : (k_pass + 1) * C_IN].bitcast(E4M3X4),
@@ -137,7 +159,7 @@ def tile_linear_pa_k_kernel(tc, x, weights, path_weights, grad_out, out):
                     stop=(k_pass == PASSES - 1),
                 )
 
-        def write_out(row, acc):
+        def scale_sums(row, acc):
             degree = DEGREE_OF_ROW[row]
             scaled = out_pool.tile([P, NODES], F32)
             nc.vector.tensor_scalar(
@@ -147,6 +169,9 @@ def tile_linear_pa_k_kernel(tc, x, weights, path_weights, grad_out, out):
                 scalar2=None,
                 op0=mybir.AluOpType.mult,
             )
+            return scaled
+
+        def store_row(row, scaled):
             back = bank_pool.tile([P, NODE_TILES, C_IN], F32, tag="bank")
             for t in range(NODE_TILES):
                 nc.tensor.transpose(back[:, t, :], scaled[:, t * P : (t + 1) * P], ident[:])
@@ -154,23 +179,29 @@ def tile_linear_pa_k_kernel(tc, x, weights, path_weights, grad_out, out):
             nc.scalar.copy(out=result[:], in_=back[:])
             nc.scalar.dma_start(out=out[:, row, :].rearrange("(t p) c -> p t c", p=P), in_=result[:])
 
-        steps = [(row, chunk) for row in range(ROWS) for chunk in range(CHUNKS)]
+        loads = loads_of_grad_out()
         w_mx = {}
         g_mx = {}
-        acc_of_row = {}
-        for i in range(len(steps) + 1):
-            if i < len(steps):
-                row, chunk = steps[i]
+        acc = None
+        finished = []
+        for i in range(len(loads) + 1):
+            if i < len(loads):
+                row, first, passes = loads[i]
                 degree = DEGREE_OF_ROW[row]
                 if degree not in w_mx:
                     w_mx[degree] = prepare_weights(degree)
-                g_mx[i] = prepare_chunk(row, chunk)
+                g_mx[i] = prepare_grad_out(row, first, passes)
+            for row, scaled in finished:
+                store_row(row, scaled)
+            finished = []
             if i >= 1:
-                row, chunk = steps[i - 1]
-                if chunk == 0:
-                    acc_of_row[row] = acc_pool.tile([P, NODES], F32, name="acc")
+                row, first, passes = loads[i - 1]
+                if first == 0:
+                    acc = acc_pool.tile([P, NODES], F32, name="acc")
                 w_codes, w_scales = w_mx[DEGREE_OF_ROW[row]]
                 g_codes, g_scales = g_mx[i - 1]
-                multiply(acc_of_row[row], chunk, w_codes, w_scales, g_codes, g_scales)
-                if chunk == CHUNKS - 1:
-                    write_out(row, acc_of_row[row])
+                multiply(acc, first, passes, w_codes, w_scales, g_codes, g_scales)
+                if first + passes == PASSES:
+                    finished.append((row, scale_sums(row, acc)))
+        for row, scaled in finished:
+            store_row(row, scaled)

@@ -26,6 +26,8 @@ NODE_TILES = NODES // P
 BLOCKS = 4
 
 LOAD_PASSES = 8
+RUN = 2
+MX_LAG = 2
 
 FLOPS = 2 * NODES * ROWS * K * C_IN
 BYTES = 2 * (DEGREES * C_IN * K + NODES * ROWS * K + DEGREES) + 4 * NODES * ROWS * C_IN
@@ -41,7 +43,7 @@ def halved_down_to_one(passes):
 
 def loads_of_grad_out():
     taper = halved_down_to_one(LOAD_PASSES)
-    loads = []
+    loads = {}
     for row in range(ROWS):
         sizes = [LOAD_PASSES] * (PASSES // LOAD_PASSES)
         if row == 0:
@@ -50,7 +52,7 @@ def loads_of_grad_out():
             sizes = sizes[:-1] + taper
         first = 0
         for passes in sizes:
-            loads.append((row, first, passes))
+            loads[(row, first)] = passes
             first += passes
     return loads
 
@@ -59,10 +61,10 @@ def tile_linear_pa_k_kernel(tc, x, weights, path_weights, grad_out, out):
     nc = tc.nc
     with ExitStack() as ctx:
         consts = ctx.enter_context(tc.tile_pool(name="consts", bufs=1))
-        w_raw_pool = ctx.enter_context(tc.tile_pool(name="w_raw", bufs=4))
+        w_raw_pool = ctx.enter_context(tc.tile_pool(name="w_raw", bufs=8))
         g_raw_pool = ctx.enter_context(tc.tile_pool(name="g_raw", bufs=4))
         grouped_pool = ctx.enter_context(tc.tile_pool(name="grouped", bufs=4))
-        g_mx_pool = ctx.enter_context(tc.tile_pool(name="g_mx", bufs=2))
+        g_mx_pool = ctx.enter_context(tc.tile_pool(name="g_mx", bufs=RUN * (MX_LAG + 2)))
         out_pool = ctx.enter_context(tc.tile_pool(name="out", bufs=2))
         bank_pool = ctx.enter_context(tc.psum_pool(name="bank", bufs=7))
         acc_pool = ctx.enter_context(tc.psum_pool(name="acc", bufs=1))
@@ -75,6 +77,31 @@ def tile_linear_pa_k_kernel(tc, x, weights, path_weights, grad_out, out):
         nc.scalar.dma_start(out=pw_bf16[:], in_=path_weights.partition_broadcast(P))
         pw = consts.tile([P, DEGREES], F32)
         nc.vector.tensor_copy(out=pw[:], in_=pw_bf16[:])
+
+        w_codes = [
+            consts.tile([P, PASSES * C_IN], U32, align_bytes=64, name="w_codes%d" % d) for d in range(DEGREES)
+        ]
+        w_scales = [
+            consts.tile([P, PASSES * C_IN], U8, align_bytes=64, name="w_scales%d" % d) for d in range(DEGREES)
+        ]
+
+        def load_weights(degree, call):
+            w_raw = w_raw_pool.tile([P, BLOCKS * K_PASS], BF16)
+            nc.sync.dma_start(
+                out=w_raw[:], in_=weights[degree, :, call * BLOCKS * K_PASS : (call + 1) * BLOCKS * K_PASS]
+            )
+            w_words = w_raw[:].bitcast(F32)
+            return [w_words[:, i * PAIRS : (i + 1) * PAIRS] for i in range(BLOCKS)]
+
+        def load_grad_out(row, first, passes):
+            g_raw = g_raw_pool.tile([P, NODE_TILES, passes * K_PASS], BF16)
+            nc.sync.dma_start(
+                out=g_raw[:],
+                in_=grad_out[:, row, first * K_PASS : (first + passes) * K_PASS].rearrange(
+                    "(t p) k -> p t k", p=P
+                ),
+            )
+            return g_raw[:].bitcast(F32)
 
         def transpose_blocks(blocks, vector_helps):
             grouped = grouped_pool.tile([P, BLOCKS * P * PACK], BF16, align_bytes=64)
@@ -94,70 +121,30 @@ def tile_linear_pa_k_kernel(tc, x, weights, path_weights, grad_out, out):
                     nc.scalar.copy(out=dst, in_=src)
             return grouped
 
-        def transpose_and_quantise(first, block_lists, codes, scales, fmt):
-            waiting = []
-            for i in range(len(block_lists)):
-                waiting.append(transpose_blocks(block_lists[i], vector_helps=((first + i) % 2 == 1)))
-                if i >= 1:
-                    nc.vector.quantize_mx(
-                        out=codes[i - 1].bitcast(fmt), scales=scales[i - 1], in_=waiting[i - 1][:]
-                    )
-            last = len(block_lists) - 1
-            nc.vector.quantize_mx(out=codes[last].bitcast(fmt), scales=scales[last], in_=waiting[last][:])
-
-        def prepare_weights(degree):
-            width = BLOCKS * C_IN
-            calls = PASSES // BLOCKS
-            w_words = []
-            for q in range(calls):
-                w_raw = w_raw_pool.tile([P, BLOCKS * K_PASS], BF16)
-                nc.sync.dma_start(
-                    out=w_raw[:], in_=weights[degree, :, q * BLOCKS * K_PASS : (q + 1) * BLOCKS * K_PASS]
-                )
-                w_words.append(w_raw[:].bitcast(F32))
-            w_codes = consts.tile([P, PASSES * C_IN], U32, align_bytes=64, name="w_codes%d" % degree)
-            w_scales = consts.tile([P, PASSES * C_IN], U8, align_bytes=64, name="w_scales%d" % degree)
-            transpose_and_quantise(
-                0,
-                [[w_words[q][:, i * PAIRS : (i + 1) * PAIRS] for i in range(BLOCKS)] for q in range(calls)],
-                [w_codes[:, q * width : (q + 1) * width] for q in range(calls)],
-                [w_scales[:, q * width : (q + 1) * width] for q in range(calls)],
-                E4M3X4,
-            )
-            return w_codes, w_scales
-
-        def prepare_grad_out(row, first, passes):
-            g_raw = g_raw_pool.tile([P, NODE_TILES, passes * K_PASS], BF16)
-            nc.sync.dma_start(
-                out=g_raw[:],
-                in_=grad_out[:, row, first * K_PASS : (first + passes) * K_PASS].rearrange(
-                    "(t p) k -> p t k", p=P
-                ),
-            )
-            g_words = g_raw[:].bitcast(F32)
-            g_codes = g_mx_pool.tile([P, passes, NODES], U32, align_bytes=64)
-            g_scales = g_mx_pool.tile([P, passes, NODES], U8, align_bytes=64)
-            transpose_and_quantise(
-                first,
-                [[g_words[:, t, c * PAIRS : (c + 1) * PAIRS] for t in range(NODE_TILES)] for c in range(passes)],
-                [g_codes[:, c, :] for c in range(passes)],
-                [g_scales[:, c, :] for c in range(passes)],
-                E5M2X4,
-            )
+        def quantise(unit, grouped):
+            kind, major, minor = unit
+            if kind == "w":
+                width = BLOCKS * C_IN
+                codes = w_codes[major][:, minor * width : (minor + 1) * width]
+                scales = w_scales[major][:, minor * width : (minor + 1) * width]
+                nc.vector.quantize_mx(out=codes.bitcast(E4M3X4), scales=scales, in_=grouped[:])
+                return None
+            g_codes = g_mx_pool.tile([P, NODES], U32, align_bytes=64)
+            g_scales = g_mx_pool.tile([P, NODES], U8, align_bytes=64)
+            nc.vector.quantize_mx(out=g_codes[:].bitcast(E5M2X4), scales=g_scales[:], in_=grouped[:])
             return g_codes, g_scales
 
-        def multiply(acc, first, passes, w_codes, w_scales, g_codes, g_scales):
-            for c in range(passes):
-                k_pass = first + c
-                nc.tensor.matmul_mx(
-                    out=acc[:],
-                    lhsT=w_codes[:, k_pass * C_IN : (k_pass + 1) * C_IN].bitcast(E4M3X4),
-                    lhsT_scale=w_scales[:, k_pass * C_IN : (k_pass + 1) * C_IN],
-                    rhs=g_codes[:, c, :].bitcast(E5M2X4),
-                    rhs_scale=g_scales[:, c, :],
-                    start=(k_pass == 0),
-                    stop=(k_pass == PASSES - 1),
-                )
+        def multiply(acc, row, k_pass, g_codes, g_scales):
+            degree = DEGREE_OF_ROW[row]
+            nc.tensor.matmul_mx(
+                out=acc[:],
+                lhsT=w_codes[degree][:, k_pass * C_IN : (k_pass + 1) * C_IN].bitcast(E4M3X4),
+                lhsT_scale=w_scales[degree][:, k_pass * C_IN : (k_pass + 1) * C_IN],
+                rhs=g_codes[:].bitcast(E5M2X4),
+                rhs_scale=g_scales[:],
+                start=(k_pass == 0),
+                stop=(k_pass == PASSES - 1),
+            )
 
         def scale_sums(row, acc):
             degree = DEGREE_OF_ROW[row]
@@ -179,29 +166,42 @@ def tile_linear_pa_k_kernel(tc, x, weights, path_weights, grad_out, out):
             nc.scalar.copy(out=result[:], in_=back[:])
             nc.scalar.dma_start(out=out[:, row, :].rearrange("(t p) c -> p t c", p=P), in_=result[:])
 
-        loads = loads_of_grad_out()
-        w_mx = {}
-        g_mx = {}
+        units = [("w", degree, call) for degree in range(DEGREES) for call in range(PASSES // BLOCKS)]
+        units += [("g", row, k_pass) for row in range(ROWS) for k_pass in range(PASSES)]
+        passes_of_load = loads_of_grad_out()
+        grouped_of = {}
+        mx_of = {}
+        g_words = None
+        g_first = 0
         acc = None
         finished = []
-        for i in range(len(loads) + 1):
-            if i < len(loads):
-                row, first, passes = loads[i]
-                degree = DEGREE_OF_ROW[row]
-                if degree not in w_mx:
-                    w_mx[degree] = prepare_weights(degree)
-                g_mx[i] = prepare_grad_out(row, first, passes)
-            for row, scaled in finished:
-                store_row(row, scaled)
-            finished = []
-            if i >= 1:
-                row, first, passes = loads[i - 1]
-                if first == 0:
-                    acc = acc_pool.tile([P, NODES], F32, name="acc")
-                w_codes, w_scales = w_mx[DEGREE_OF_ROW[row]]
-                g_codes, g_scales = g_mx[i - 1]
-                multiply(acc, first, passes, w_codes, w_scales, g_codes, g_scales)
-                if first + passes == PASSES:
-                    finished.append((row, scale_sums(row, acc)))
+        for s in range(len(units) + RUN * MX_LAG):
+            if s < len(units):
+                kind, major, minor = units[s]
+                if kind == "w":
+                    blocks = load_weights(major, minor)
+                else:
+                    if (major, minor) in passes_of_load:
+                        g_words = load_grad_out(major, minor, passes_of_load[(major, minor)])
+                        g_first = minor
+                    c = minor - g_first
+                    blocks = [g_words[:, t, c * PAIRS : (c + 1) * PAIRS] for t in range(NODE_TILES)]
+                grouped_of[s] = transpose_blocks(blocks, vector_helps=(s % 2 == 1))
+            if 1 <= s <= len(units):
+                mx_of[s - 1] = quantise(units[s - 1], grouped_of[s - 1])
+            if s % RUN == RUN - 1:
+                for row, scaled in finished:
+                    store_row(row, scaled)
+                finished = []
+                newest = s - RUN * MX_LAG
+                for u in range(max(newest - RUN + 1, 0), newest + 1):
+                    kind, row, k_pass = units[u]
+                    if kind == "g":
+                        if k_pass == 0:
+                            acc = acc_pool.tile([P, NODES], F32, name="acc")
+                        g_codes, g_scales = mx_of[u]
+                        multiply(acc, row, k_pass, g_codes, g_scales)
+                        if k_pass == PASSES - 1:
+                            finished.append((row, scale_sums(row, acc)))
         for row, scaled in finished:
             store_row(row, scaled)

from contextlib import ExitStack

import concourse.mybir as mybir
from concourse.masks import make_identity

BF16 = mybir.dt.bfloat16
F32 = mybir.dt.float32
U32 = mybir.dt.uint32
U8 = mybir.dt.uint8
E4M3X4 = mybir.dt.float8_e4m3fn_x4
E5M2X4 = mybir.dt.float8_e5m2_x4

P = 128
PACK = 4
K_PASS = P * PACK
PAIRS = K_PASS // 2

NODES = 512
ROWS = 4
DEGREE_OF_ROW = [0, 1, 1, 1]
DEGREES = 2
C_IN = 128
K = 8192
PASSES = K // K_PASS
NODE_TILES = NODES // P
BLOCKS = 4

LOAD_PASSES = 8
RUN = 2
MX_LAG = 2

FLOPS = 2 * NODES * ROWS * K * C_IN
BYTES = 2 * (DEGREES * C_IN * K + NODES * ROWS * K + DEGREES) + 4 * NODES * ROWS * C_IN


def halved_down_to_one(passes):
    pieces = []
    while passes > 1:
        passes //= 2
        pieces.append(passes)
    return pieces + [1]


def loads_of_grad_out():
    taper = halved_down_to_one(LOAD_PASSES)
    loads = {}
    for row in range(ROWS):
        sizes = [LOAD_PASSES] * (PASSES // LOAD_PASSES)
        if row == 0:
            sizes = list(reversed(taper)) + sizes[1:]
        if row == ROWS - 1:
            sizes = sizes[:-1] + taper
        first = 0
        for passes in sizes:
            loads[(row, first)] = passes
            first += passes
    return loads


def tile_linear_pa_k_kernel(tc, x, weights, path_weights, grad_out, out):
    nc = tc.nc
    with ExitStack() as ctx:
        consts = ctx.enter_context(tc.tile_pool(name="consts", bufs=1))
        w_raw_pool = ctx.enter_context(tc.tile_pool(name="w_raw", bufs=8))
        g_raw_pool = ctx.enter_context(tc.tile_pool(name="g_raw", bufs=4))
        grouped_pool = ctx.enter_context(tc.tile_pool(name="grouped", bufs=4))
        g_mx_pool = ctx.enter_context(tc.tile_pool(name="g_mx", bufs=RUN * (MX_LAG + 2)))
        out_pool = ctx.enter_context(tc.tile_pool(name="out", bufs=2))
        bank_pool = ctx.enter_context(tc.psum_pool(name="bank", bufs=7))
        acc_pool = ctx.enter_context(tc.psum_pool(name="acc", bufs=1))
        ctx.enter_context(tc.manual_schedule())

        ident = consts.tile([P, P], F32)
        make_identity(nc, ident[:])

        pw_bf16 = consts.tile([P, DEGREES], BF16)
        nc.scalar.dma_start(out=pw_bf16[:], in_=path_weights.partition_broadcast(P))
        pw = consts.tile([P, DEGREES], F32)
        nc.vector.tensor_copy(out=pw[:], in_=pw_bf16[:])

        w_codes = [
            consts.tile([P, PASSES * C_IN], U32, align_bytes=64, name="w_codes%d" % d) for d in range(DEGREES)
        ]
        w_scales = [
            consts.tile([P, PASSES * C_IN], U8, align_bytes=64, name="w_scales%d" % d) for d in range(DEGREES)
        ]

        def load_weights(degree, call):
            w_raw = w_raw_pool.tile([P, BLOCKS * K_PASS], BF16)
            nc.sync.dma_start(
                out=w_raw[:], in_=weights[degree, :, call * BLOCKS * K_PASS : (call + 1) * BLOCKS * K_PASS]
            )
            w_words = w_raw[:].bitcast(F32)
            return [w_words[:, i * PAIRS : (i + 1) * PAIRS] for i in range(BLOCKS)]

        def load_grad_out(row, first, passes):
            g_raw = g_raw_pool.tile([P, NODE_TILES, passes * K_PASS], BF16)
            nc.sync.dma_start(
                out=g_raw[:],
                in_=grad_out[:, row, first * K_PASS : (first + passes) * K_PASS].rearrange(
                    "(t p) k -> p t k", p=P
                ),
            )
            return g_raw[:].bitcast(F32)

        def transpose_blocks(blocks, vector_helps):
            grouped = grouped_pool.tile([P, BLOCKS * P * PACK], BF16, align_bytes=64)
            grouped_words = grouped[:].bitcast(F32).rearrange("p (b r u) -> p b r u", b=BLOCKS, u=2)
            for half in range(2):
                bank = bank_pool.tile([P, 2, 2, P], F32, tag="bank")
                for b in range(2):
                    for u in range(2):
                        nc.tensor.transpose(
                            bank[:, b, u, :], blocks[2 * half + b][:, u * P : (u + 1) * P], ident[:]
                        )
                dst = grouped_words[:, 2 * half : 2 * half + 2, :, :]
                src = bank[:].rearrange("p b u r -> p b r u")
                if half == 1 and vector_helps:
                    nc.vector.tensor_copy(out=dst, in_=src)
                else:
                    nc.scalar.copy(out=dst, in_=src)
            return grouped

        def quantise(unit, grouped):
            kind, major, minor = unit
            if kind == "w":
                width = BLOCKS * C_IN
                codes = w_codes[major][:, minor * width : (minor + 1) * width]
                scales = w_scales[major][:, minor * width : (minor + 1) * width]
                nc.vector.quantize_mx(out=codes.bitcast(E4M3X4), scales=scales, in_=grouped[:])
                return None
            g_codes = g_mx_pool.tile([P, NODES], U32, align_bytes=64)
            g_scales = g_mx_pool.tile([P, NODES], U8, align_bytes=64)
            nc.vector.quantize_mx(out=g_codes[:].bitcast(E5M2X4), scales=g_scales[:], in_=grouped[:])
            return g_codes, g_scales

        def multiply(acc, row, k_pass, g_codes, g_scales):
            degree = DEGREE_OF_ROW[row]
            nc.tensor.matmul_mx(
                out=acc[:],
                lhsT=w_codes[degree][:, k_pass * C_IN : (k_pass + 1) * C_IN].bitcast(E4M3X4),
                lhsT_scale=w_scales[degree][:, k_pass * C_IN : (k_pass + 1) * C_IN],
                rhs=g_codes[:].bitcast(E5M2X4),
                rhs_scale=g_scales[:],
                start=(k_pass == 0),
                stop=(k_pass == PASSES - 1),
            )

        def scale_sums(row, acc):
            degree = DEGREE_OF_ROW[row]
            scaled = out_pool.tile([P, NODES], F32)
            nc.vector.tensor_scalar(
                out=scaled[:],
                in0=acc[:],
                scalar1=pw[:, degree : degree + 1],
                scalar2=None,
                op0=mybir.AluOpType.mult,
            )
            return scaled

        def store_row(row, scaled):
            back = bank_pool.tile([P, NODE_TILES, C_IN], F32, tag="bank")
            for t in range(NODE_TILES):
                nc.tensor.transpose(back[:, t, :], scaled[:, t * P : (t + 1) * P], ident[:])
            result = out_pool.tile([P, NODE_TILES, C_IN], F32)
            nc.scalar.copy(out=result[:], in_=back[:])
            nc.scalar.dma_start(out=out[:, row, :].rearrange("(t p) c -> p t c", p=P), in_=result[:])

        units = [("w", degree, call) for degree in range(DEGREES) for call in range(PASSES // BLOCKS)]
        units += [("g", row, k_pass) for row in range(ROWS) for k_pass in range(PASSES)]
        passes_of_load = loads_of_grad_out()
        grouped_of = {}
        mx_of = {}
        g_words = None
        g_first = 0
        acc = None
        finished = []
        for s in range(len(units) + RUN * MX_LAG):
            if s < len(units):
                kind, major, minor = units[s]
                if kind == "w":
                    blocks = load_weights(major, minor)
                else:
                    if (major, minor) in passes_of_load:
                        g_words = load_grad_out(major, minor, passes_of_load[(major, minor)])
                        g_first = minor
                    c = minor - g_first
                    blocks = [g_words[:, t, c * PAIRS : (c + 1) * PAIRS] for t in range(NODE_TILES)]
                grouped_of[s] = transpose_blocks(blocks, vector_helps=(s % 2 == 1))
            if 1 <= s <= len(units):
                mx_of[s - 1] = quantise(units[s - 1], grouped_of[s - 1])
            if s % RUN == RUN - 1:
                for row, scaled in finished:
                    store_row(row, scaled)
                finished = []
                newest = s - RUN * MX_LAG
                for u in range(max(newest - RUN + 1, 0), newest + 1):
                    kind, row, k_pass = units[u]
                    if kind == "g":
                        if k_pass == 0:
                            acc = acc_pool.tile([P, NODES], F32, name="acc")
                        g_codes, g_scales = mx_of[u]
                        multiply(acc, row, k_pass, g_codes, g_scales)
                        if k_pass == PASSES - 1:
                            finished.append((row, scale_sums(row, acc)))
        for row, scaled in finished:
            store_row(row, scaled)
